import numpy as np
import ml_dtypes


def mxq(x, axis, fmt="e4m3"):
    dtype, down = {"e4m3": (ml_dtypes.float8_e4m3fn, 7), "e5m2": (ml_dtypes.float8_e5m2, 14)}[fmt]
    v = np.moveaxis(np.asarray(x, np.float32).astype(ml_dtypes.bfloat16).astype(np.float64), axis, -1)
    blocks = v.reshape(v.shape[:-1] + (-1, 32))
    amax = np.abs(blocks).max(-1, keepdims=True)
    byte = np.maximum(np.where(amax > 0, np.frexp(amax)[1] - 1 + 127, 0) - down, 1)
    scale = np.exp2(byte - 127.0)
    codes = (blocks / scale).astype(np.float32).astype(dtype).astype(np.float64)
    return np.moveaxis((codes * scale).reshape(v.shape), -1, axis)


WIDE = False


def mx_kscale(k):
    if not WIDE:
        return np.ones(k)
    levels = np.array([10, -10, 5, -5, 0])
    a = np.random.permutation(np.resize(levels, k // 512 * 4)).reshape(k // 512, 4)
    idx = np.arange(k)
    return np.exp2(a[idx // 512, idx % 128 // 32])


BF16 = ml_dtypes.bfloat16


def bf(x):
    return np.asarray(x, np.float32).astype(BF16)


def f64(x):
    return np.asarray(x).astype(np.float64)


EPS = 1e-12
N, C, H, W = 16, 512, 32, 32
K_ALL = 128
K_CLUSTERS = 127


def _l2norm(v, axis):
    n = np.sqrt(np.sum(v * v, axis=axis, keepdims=True))
    return v / np.maximum(n, EPS)


def _softmax(v, axis):
    e = np.exp(v - v.max(axis=axis, keepdims=True))
    return e / e.sum(axis=axis, keepdims=True)


def setup_inputs():
    s = mx_kscale(C)
    g = np.exp2(np.round(np.log2(np.sqrt(np.mean(s * s)))))
    return {"x": bf(np.random.standard_normal((N, C, H, W)) * s[None, :, None, None]),
            "conv_w": bf(np.random.standard_normal((K_ALL, C)) * g / s[None, :]),
            "conv_b": bf(np.random.standard_normal(K_ALL) * 0.1),
            "centroids": bf(np.random.standard_normal((K_ALL, C)) * 0.003 * s[None, :] / g)}


def reference(x, conv_w, conv_b, centroids):
    x = f64(x)
    n_, c_, h_, w_ = x.shape
    xn = _l2norm(x, 1)
    xf = xn.reshape(n_, c_, h_ * w_)
    logits = (mxq(f64(conv_w), 1, "e4m3") @ mxq(xf, 1, "e4m3")) + f64(conv_b)[None, :, None]
    a = _softmax(logits, 1)
    vlad = (mxq(a, 2, "e4m3") @ mxq(xf, 2, "e4m3").transpose(0, 2, 1)) - np.sum(a, axis=2)[:, :, None] * f64(centroids)[None]
    vlad = vlad[:, :K_CLUSTERS, :]
    vlad = _l2norm(vlad, 2)
    flat = vlad.reshape(n_, -1)
    return _l2norm(flat, 1)

@@ -1,0 +1,383 @@
+from contextlib import ExitStack
+
+import concourse.bass as bass
+import concourse.mybir as mybir
+import concourse.tile as tile
+from concourse.masks import make_identity
+
+F32 = mybir.dt.float32
+BF16 = mybir.dt.bfloat16
+U32 = mybir.dt.uint32
+U8 = mybir.dt.uint8
+FP8X4 = mybir.dt.float8_e4m3fn_x4
+ALU = mybir.AluOpType
+ACT = mybir.ActivationFunctionType
+AX = mybir.AxisListType
+
+P = 128
+N_IMG = 16
+C = 512
+PX = 1024
+NU = 2 * N_IMG
+TINY = 1e-24
+FLOPS = 2 * 2 * N_IMG * 128 * C * PX
+PIN = True
+
+
+def tile_netvlad_kernel(tc, x, conv_w, conv_b, centroids, out):
+    nc = tc.nc
+    with ExitStack() as ctx:
+        const = ctx.enter_context(tc.tile_pool(name="const", bufs=1))
+        xpool = ctx.enter_context(tc.tile_pool(name="xpool", bufs=4))
+        big = ctx.enter_context(tc.tile_pool(name="big", bufs=2))
+        keep = ctx.enter_context(tc.tile_pool(name="keep", bufs=4))
+        soft = ctx.enter_context(tc.tile_pool(name="soft", bufs=3))
+        small = ctx.enter_context(tc.tile_pool(name="small", bufs=6))
+        ps_r = ctx.enter_context(tc.psum_pool(name="ps_r", bufs=4))
+        ps_b = ctx.enter_context(tc.psum_pool(name="ps_b", bufs=1))
+        ps_l = ctx.enter_context(tc.psum_pool(name="ps_l", bufs=1))
+        ps_v = ctx.enter_context(tc.psum_pool(name="ps_v", bufs=1))
+        ps_m = ctx.enter_context(tc.psum_pool(name="ps_m", bufs=1))
+        if PIN:
+            ctx.enter_context(tc.manual_schedule())
+
+        xs = {}
+
+        def load(n):
+            if n >= N_IMG:
+                return
+            xt = xpool.tile([P, 4 * PX], BF16, name="xt%d" % n, tag="xt")
+            nc.sync.dma_start(out=xt[:], in_=x[n].rearrange("(q j) h w -> q (j h w)", j=4))
+            xs[n] = xt
+
+        w_sb = const.tile([P, C], BF16, name="w_sb")
+        nc.sync.dma_start(out=w_sb[:], in_=conv_w)
+        load(0)
+        b_bc = const.tile([P, 128], BF16, name="b_bc")
+        nc.sync.dma_start(out=b_bc[:], in_=conv_b.partition_broadcast(P))
+        cent = const.tile([P, C], BF16, name="cent")
+        nc.sync.dma_start(out=cent[:], in_=centroids)
+        load(1)
+        load(2)
+        load(3)
+
+        ident = const.tile([P, P], F32, name="ident")
+        make_identity(nc, ident[:])
+        neghalf = const.tile([P, 4], F32, name="neghalf")
+        nc.gpsimd.memset(neghalf[:], -0.5)
+        onesm = const.tile([P, P], F32, name="onesm")
+        nc.vector.tensor_scalar(
+            out=onesm[:], in0=ident[:, 127:128].to_broadcast([P, P]),
+            scalar1=-1.0, scalar2=1.0, op0=ALU.mult, op1=ALU.add,
+        )
+        junk = const.tile([P, 256], BF16, name="junk")
+        junk2 = const.tile([P, C], BF16, name="junk2")
+        misc = ps_m.tile([P, 512], F32, name="misc")
+
+        w32 = w_sb[:].bitcast(F32)
+        w_t = ps_r.tile([P, 512], F32, name="w_t", tag="R")
+        for v in range(2):
+            nc.tensor.transpose(w_t[:, v * 128:(v + 1) * 128], w32[:, v:256:2], ident[:])
+        wg = const.tile([P, C], BF16, name="wg", align_bytes=64)
+        nc.vector.tensor_copy(
+            out=wg[:].bitcast(F32).rearrange("p (k v) -> p k v", v=2),
+            in_=w_t[:, 0:256].rearrange("p (v k) -> p k v", v=2),
+        )
+        w_codes = const.tile([P, 128], U32, name="w_codes", align_bytes=64)
+        w_scales = const.tile([P, 128], U8, name="w_scales", align_bytes=64)
+        nc.vector.quantize_mx(out=w_codes[:].bitcast(FP8X4), scales=w_scales[:], in_=wg[:])
+
+        st = {}
+
+        def ok(s):
+            return 0 <= s < NU
+
+        def do_t(s):
+            if not ok(s):
+                return
+            n, g = divmod(s, 2)
+            x32 = xs[n][:].bitcast(F32)
+            banks = []
+            for h in range(2):
+                rh = ps_r.tile([P, 512], F32, name="r%d_%d" % (s, h), tag="R")
+                for u in range(2):
+                    for jj in range(2):
+                        j = 2 * h + jj
+                        col = j * 512 + 256 * g + 128 * u
+                        nc.tensor.transpose(
+                            rh[:, u * 256 + jj * 128:u * 256 + (jj + 1) * 128],
+                            x32[:, col:col + 128], ident[:],
+                        )
+                banks.append(rh)
+            st[("R", s)] = banks
+
+        def do_ss(s):
+            if not ok(s):
+                return
+            ssp = small.tile([P, 8], F32, name="ssp%d" % s, tag="ssp")
+            for h in range(2):
+                r16 = st[("R", s)][h][:].bitcast(BF16).rearrange("p (u c e) -> p u c e", u=2, e=2)
+                for u in range(2):
+                    for e in range(2):
+                        k = 4 * h + 2 * u + e
+                        nc.scalar.activation(
+                            out=junk[:], in_=r16[:, u, :, e], func=ACT.Square,
+                            accum_out=ssp[:, k:k + 1],
+                        )
+            st[("ssp", s)] = ssp
+
+        def do_ssadd(s):
+            if not ok(s):
+                return
+            ssp = st[("ssp", s)]
+            ss = small.tile([P, 4], F32, name="ss%d" % s, tag="ss")
+            nc.vector.tensor_tensor(out=ss[:], in0=ssp[:, 0:4], in1=ssp[:, 4:8], op=ALU.add)
+            ssc = small.tile([P, 4], F32, name="ssc%d" % s, tag="ssc")
+            nc.vector.tensor_scalar_max(out=ssc[:], in0=ss[:], scalar1=TINY)
+            st[("ssc", s)] = ssc
+
+        def do_pow(s):
+            if not ok(s):
+                return
+            rn = small.tile([P, 4], F32, name="rn%d" % s, tag="rn")
+            nc.gpsimd.tensor_tensor(out=rn[:], in0=st[("ssc", s)][:], in1=neghalf[:], op=ALU.pow)
+            st[("rn", s)] = rn
+
+        def do_b(s):
+            if not ok(s):
+                return
+            rn = st[("rn", s)]
+            bt = ps_b.tile([P, 512], F32, name="bt%d" % s, tag="B")
+            for t in range(4):
+                nc.tensor.transpose(
+                    bt[:, t * 128:(t + 1) * 128], rn[:, t:t + 1].to_broadcast([P, P]), ident[:]
+                )
+            st[("B", s)] = bt
+
+        def do_n2(s):
+            if not ok(s):
+                return
+            rn = st[("rn", s)]
+            xg = big.tile([P, 2048], BF16, name="xg%d" % s, tag="xg", align_bytes=64)
+            xg4 = xg[:].rearrange("p (c u e) -> p c u e", u=2, e=2)
+            rn4 = rn[:].rearrange("p (u e) -> p u e", u=2).unsqueeze(1).to_broadcast([P, 256, 2, 2])
+            for h in range(2):
+                r16 = st[("R", s)][h][:].bitcast(BF16).rearrange("p (u c e) -> p c u e", u=2, e=2)
+                nc.vector.tensor_tensor(
+                    out=xg4[:, 256 * h:256 * (h + 1)], in0=r16, in1=rn4, op=ALU.mult
+                )
+            st[("xg", s)] = xg
+
+        def do_n1(s):
+            if not ok(s):
+                return
+            n, g = divmod(s, 2)
+            cg = big.tile([P, 2048], BF16, name="cg%d" % s, tag="cg", align_bytes=64)
+            cg4 = cg[:].rearrange("p (t q j) -> p t q j", t=4, j=4)
+            xv = xs[n][:].rearrange("p (j g u q e) -> p g u e q j", j=4, g=2, u=2, e=2)
+            b3 = st[("B", s)][:].rearrange("p (t q) -> p t q", t=4)
+            for u in range(2):
+                nc.vector.tensor_tensor(
+                    out=cg4[:, 2 * u:2 * u + 2],
+                    in0=xv[:, g, u],
+                    in1=b3[:, 2 * u:2 * u + 2, :].unsqueeze(3).to_broadcast([P, 2, 128, 4]),
+                    op=ALU.mult,
+                )
+            st[("cg", s)] = cg
+
+        def do_qp(s):
+            if not ok(s):
+                return
+            xpc = keep.tile([P, 512], U32, name="xpc%d" % s, tag="xpc", align_bytes=64)
+            xps = keep.tile([P, 512], U8, name="xps%d" % s, tag="xps", align_bytes=64)
+            nc.vector.quantize_mx(out=xpc[:].bitcast(FP8X4), scales=xps[:], in_=st[("xg", s)][:])
+            st[("xp", s)] = (xpc, xps)
+
+        def do_qc(s):
+            if not ok(s):
+                return
+            xcc = big.tile([P, 512], U32, name="xcc%d" % s, tag="xcc", align_bytes=64)
+            xcs = big.tile([P, 512], U8, name="xcs%d" % s, tag="xcs", align_bytes=64)
+            nc.vector.quantize_mx(out=xcc[:].bitcast(FP8X4), scales=xcs[:], in_=st[("cg", s)][:])
+            st[("xc", s)] = (xcc, xcs)
+
+        def do_mx1(s):
+            if not ok(s):
+                return
+            xcc, xcs = st[("xc", s)]
+            lt = ps_l.tile([P, 512], F32, name="lt%d" % s, tag="L")
+            for t in range(4):
+                cols = slice(t * 128, (t + 1) * 128)
+                nc.tensor.matmul_mx(
+                    out=lt[:, cols],
+                    lhsT=xcc[:, cols].bitcast(FP8X4), lhsT_scale=xcs[:, cols],
+                    rhs=w_codes[:].bitcast(FP8X4), rhs_scale=w_scales[:],
+                    start=True, stop=True,
+                )
+            st[("L", s)] = lt
+
+        def do_addmax(s):
+            if not ok(s):
+                return
+            z = soft.tile([P, 512], F32, name="z%d" % s, tag="z")
+            z3 = z[:].rearrange("p (t k) -> p t k", t=4)
+            nc.vector.tensor_tensor(
+                out=z3, in0=st[("L", s)][:].rearrange("p (t k) -> p t k", t=4),
+                in1=b_bc[:].unsqueeze(1).to_broadcast([P, 4, 128]), op=ALU.add,
+            )
+            negm = small.tile([P, 4], F32, name="negm%d" % s, tag="negm")
+            nc.vector.tensor_reduce(out=negm[:], in_=z3, axis=AX.X, op=ALU.max, negate=True)
+            st[("z", s)] = (z, negm)
+
+        def do_exp(s):
+            if not ok(s):
+                return
+            z, negm = st[("z", s)]
+            ex = soft.tile([P, 512], F32, name="ex%d" % s, tag="ex")
+            sums = small.tile([P, 4], F32, name="sums%d" % s, tag="sums")
+            for t in range(4):
+                cols = slice(t * 128, (t + 1) * 128)
+                nc.scalar.activation(
+                    out=ex[:, cols], in_=z[:, cols], func=ACT.Exp,
+                    bias=negm[:, t:t + 1], scale=1.0, accum_out=sums[:, t:t + 1],
+                )
+            st[("ex", s)] = (ex, sums)
+
+        def do_a(s):
+            if not ok(s):
+                return
+            ex, sums = st[("ex", s)]
+            rs = small.tile([P, 4], F32, name="rs%d" % s, tag="rs")
+            nc.vector.reciprocal(out=rs[:], in_=sums[:])
+            ag = big.tile([P, 512], BF16, name="ag%d" % s, tag="ag", align_bytes=64)
+            nc.vector.tensor_tensor(
+                out=ag[:].rearrange("p (k t) -> p k t", t=4),
+                in0=ex[:].rearrange("p (t k) -> p k t", t=4),
+                in1=rs[:].unsqueeze(1).to_broadcast([P, 128, 4]), op=ALU.mult,
+            )
+            st[("rs", s)] = rs
+            st[("ag", s)] = ag
+
+        def do_qa(s):
+            if not ok(s):
+                return
+            ac = big.tile([P, 128], U32, name="ac%d" % s, tag="ac", align_bytes=64)
+            asc = big.tile([P, 128], U8, name="asc%d" % s, tag="asc", align_bytes=64)
+            nc.vector.quantize_mx(out=ac[:].bitcast(FP8X4), scales=asc[:], in_=st[("ag", s)][:])
+            st[("a", s)] = (ac, asc)
+
+        def do_mx2(s):
+            if not ok(s):
+                return
+            n, g = divmod(s, 2)
+            ex, sums = st[("ex", s)]
+            rs = st[("rs", s)]
+            col = 4 * (n % 2) + g
+            for t in range(4):
+                nc.tensor.matmul(
+                    out=misc[:, col:col + 1], lhsT=ex[:, t * 128:(t + 1) * 128],
+                    rhs=rs[:, t:t + 1], start=(t == 0), stop=(t == 3),
+                )
+            if g == 0:
+                st[("V", n)] = ps_v.tile([P, 512], F32, name="vl%d" % n, tag="V")
+            ac, asc = st[("a", s)]
+            xpc, xps = st[("xp", s)]
+            nc.tensor.matmul_mx(
+                out=st[("V", n)][:],
+                lhsT=ac[:].bitcast(FP8X4), lhsT_scale=asc[:],
+                rhs=xpc[:].bitcast(FP8X4), rhs_scale=xps[:],
+                start=(g == 0), stop=(g == 1),
+            )
+
+        def img(num):
+            if num % 2 == 0 and 0 <= num // 2 < N_IMG:
+                return num // 2
+            return None
+
+        def fin_a(n):
+            c0 = 4 * (n % 2)
+            nas = small.tile([P, 1], F32, name="nas%d" % n, tag="nas")
+            nc.vector.tensor_reduce(out=nas[:], in_=misc[:, c0:c0 + 2], axis=AX.X, op=ALU.add, negate=True)
+            vv = soft.tile([P, C], F32, name="vv%d" % n, tag="vv")
+            nc.vector.scalar_tensor_tensor(
+                out=vv[:].rearrange("p (q j) -> p q j", j=4),
+                in0=cent[:].rearrange("p (q j) -> p q j", j=4),
+                scalar=nas[:, 0:1],
+                in1=st[("V", n)][:].rearrange("p (j q) -> p q j", j=4),
+                op0=ALU.mult, op1=ALU.add,
+            )
+            ssr = small.tile([P, 1], F32, name="ssr%d" % n, tag="ssr")
+            nc.scalar.activation(out=junk2[:], in_=vv[:], func=ACT.Square, accum_out=ssr[:])
+            st[("vv", n)] = vv
+            st[("ssr", n)] = ssr
+
+        def fin_clamp_r(n):
+            src = small.tile([P, 1], F32, name="src%d" % n, tag="src")
+            nc.vector.tensor_scalar_max(out=src[:], in0=st[("ssr", n)][:], scalar1=TINY)
+            st[("src", n)] = src
+
+        def fin_pow_r(n):
+            rk = small.tile([P, 1], F32, name="rk%d" % n, tag="rk")
+            nc.gpsimd.tensor_tensor(out=rk[:], in0=st[("src", n)][:], in1=neghalf[:, 0:1], op=ALU.pow)
+            st[("rk", n)] = rk
+
+        def fin_gsum(n):
+            rk = st[("rk", n)]
+            val = small.tile([P, 1], F32, name="val%d" % n, tag="val")
+            nc.vector.scalar_tensor_tensor(
+                out=val[:], in0=st[("ssr", n)][:], scalar=rk[:, 0:1], in1=rk[:],
+                op0=ALU.mult, op1=ALU.mult,
+            )
+            c0 = 4 * (n % 2) + 2
+            nc.tensor.matmul(out=misc[:, c0:c0 + 1], lhsT=onesm[:], rhs=val[:], start=True, stop=True)
+
+        def fin_clamp_g(n):
+            c0 = 4 * (n % 2) + 2
+            gs = small.tile([P, 1], F32, name="gs%d" % n, tag="gs")
+            nc.vector.tensor_scalar_max(out=gs[:], in0=misc[:, c0:c0 + 1], scalar1=TINY)
+            st[("gs", n)] = gs
+
+        def fin_out(n):
+            rg = small.tile([P, 1], F32, name="rg%d" % n, tag="rg")
+            nc.gpsimd.tensor_tensor(out=rg[:], in0=st[("gs", n)][:], in1=neghalf[:, 0:1], op=ALU.pow)
+            ot = soft.tile([P, C], F32, name="ot%d" % n, tag="ot")
+            nc.gpsimd.tensor_scalar(
+                out=ot[:], in0=st[("vv", n)][:], scalar1=st[("rk", n)][:, 0:1], scalar2=rg[:, 0:1],
+                op0=ALU.mult, op1=ALU.mult,
+            )
+            o2 = out[n].rearrange("(k c) -> k c", c=C)
+            nc.sync.dma_start(out=o2[0:112, :], in_=ot[0:112, :])
+            nc.sync.dma_start(out=o2[112:127, :], in_=ot[112:127, :])
+
+        for s in range(-2, NU + 4):
+            na = img(s - 4)
+            nb = img(s - 5)
+            if na is not None:
+                fin_a(na)
+            do_n2(s)
+            do_t(s + 2)
+            do_ss(s + 2)
+            do_n1(s)
+            if s >= 0 and s % 2 == 1:
+                load(s // 2 + 4)
+            do_ssadd(s + 1)
+            if na is not None:
+                fin_clamp_r(na)
+            if nb is not None:
+                fin_clamp_g(nb)
+            do_pow(s + 1)
+            if na is not None:
+                fin_pow_r(na)
+            if nb is not None:
+                fin_out(nb)
+            do_b(s + 1)
+            do_qp(s)
+            do_addmax(s - 1)
+            do_exp(s - 1)
+            if na is not None:
+                fin_gsum(na)
+            do_qc(s)
+            do_mx1(s)
+            do_a(s - 2)
+            do_qa(s - 2)
+            do_mx2(s - 2)

@@ -1,8 +1,6 @@
 from contextlib import ExitStack
 
-import concourse.bass as bass
 import concourse.mybir as mybir
-import concourse.tile as tile
 from concourse.masks import make_identity
 
 F32 = mybir.dt.float32
@@ -21,7 +19,6 @@ PX = 1024
 NU = 2 * N_IMG
 TINY = 1e-24
 FLOPS = 2 * 2 * N_IMG * 128 * C * PX
-PIN = True
 
 
 def tile_netvlad_kernel(tc, x, conv_w, conv_b, centroids, out):
@@ -30,7 +27,7 @@ def tile_netvlad_kernel(tc, x, conv_w, conv_b, centroids, out):
         const = ctx.enter_context(tc.tile_pool(name="const", bufs=1))
         xpool = ctx.enter_context(tc.tile_pool(name="xpool", bufs=4))
         big = ctx.enter_context(tc.tile_pool(name="big", bufs=2))
-        keep = ctx.enter_context(tc.tile_pool(name="keep", bufs=4))
+        keep = ctx.enter_context(tc.tile_pool(name="keep", bufs=5))
         soft = ctx.enter_context(tc.tile_pool(name="soft", bufs=3))
         small = ctx.enter_context(tc.tile_pool(name="small", bufs=6))
         ps_r = ctx.enter_context(tc.psum_pool(name="ps_r", bufs=4))
@@ -38,8 +35,7 @@ def tile_netvlad_kernel(tc, x, conv_w, conv_b, centroids, out):
         ps_l = ctx.enter_context(tc.psum_pool(name="ps_l", bufs=1))
         ps_v = ctx.enter_context(tc.psum_pool(name="ps_v", bufs=1))
         ps_m = ctx.enter_context(tc.psum_pool(name="ps_m", bufs=1))
-        if PIN:
-            ctx.enter_context(tc.manual_schedule())
+        ctx.enter_context(tc.manual_schedule())
 
         xs = {}
 
@@ -63,15 +59,18 @@ def tile_netvlad_kernel(tc, x, conv_w, conv_b, centroids, out):
 
         ident = const.tile([P, P], F32, name="ident")
         make_identity(nc, ident[:])
-        neghalf = const.tile([P, 4], F32, name="neghalf")
-        nc.gpsimd.memset(neghalf[:], -0.5)
+        expo_a = const.tile([P, 4], F32, name="expo_a")
+        nc.gpsimd.memset(expo_a[:], -0.5)
+        expo_b = const.tile([P, 5], F32, name="expo_b")
+        nc.gpsimd.memset(expo_b[:, 0:4], -1.0)
+        nc.gpsimd.memset(expo_b[:, 4:5], -0.5)
         onesm = const.tile([P, P], F32, name="onesm")
         nc.vector.tensor_scalar(
             out=onesm[:], in0=ident[:, 127:128].to_broadcast([P, P]),
             scalar1=-1.0, scalar2=1.0, op0=ALU.mult, op1=ALU.add,
         )
-        junk = const.tile([P, 256], BF16, name="junk")
-        junk2 = const.tile([P, C], BF16, name="junk2")
+        junk = const.tile([P, C], BF16, name="junk")
+        junk3 = const.tile([P, 2], F32, name="junk3")
         misc = ps_m.tile([P, 512], F32, name="misc")
 
         w32 = w_sb[:].bitcast(F32)
@@ -92,60 +91,54 @@ def tile_netvlad_kernel(tc, x, conv_w, conv_b, centroids, out):
         def ok(s):
             return 0 <= s < NU
 
+        def img(num):
+            if num % 2 == 0 and 0 <= num // 2 < N_IMG:
+                return num // 2
+            return None
+
+        def r16(s, u):
+            return st[("R", s)][u][:].bitcast(BF16).rearrange("p (c e) -> p c e", e=2)
+
         def do_t(s):
-            if not ok(s):
-                return
             n, g = divmod(s, 2)
             x32 = xs[n][:].bitcast(F32)
             banks = []
-            for h in range(2):
-                rh = ps_r.tile([P, 512], F32, name="r%d_%d" % (s, h), tag="R")
-                for u in range(2):
-                    for jj in range(2):
-                        j = 2 * h + jj
-                        col = j * 512 + 256 * g + 128 * u
-                        nc.tensor.transpose(
-                            rh[:, u * 256 + jj * 128:u * 256 + (jj + 1) * 128],
-                            x32[:, col:col + 128], ident[:],
-                        )
-                banks.append(rh)
+            for u in range(2):
+                ru = ps_r.tile([P, 512], F32, name="r%d_%d" % (s, u), tag="R")
+                for j in range(4):
+                    col = j * 512 + 256 * g + 128 * u
+                    nc.tensor.transpose(ru[:, j * 128:(j + 1) * 128], x32[:, col:col + 128], ident[:])
+                banks.append(ru)
             st[("R", s)] = banks
 
         def do_ss(s):
-            if not ok(s):
-                return
-            ssp = small.tile([P, 8], F32, name="ssp%d" % s, tag="ssp")
-            for h in range(2):
-                r16 = st[("R", s)][h][:].bitcast(BF16).rearrange("p (u c e) -> p u c e", u=2, e=2)
-                for u in range(2):
-                    for e in range(2):
-                        k = 4 * h + 2 * u + e
-                        nc.scalar.activation(
-                            out=junk[:], in_=r16[:, u, :, e], func=ACT.Square,
-                            accum_out=ssp[:, k:k + 1],
-                        )
-            st[("ssp", s)] = ssp
-
-        def do_ssadd(s):
-            if not ok(s):
-                return
-            ssp = st[("ssp", s)]
-            ss = small.tile([P, 4], F32, name="ss%d" % s, tag="ss")
-            nc.vector.tensor_tensor(out=ss[:], in0=ssp[:, 0:4], in1=ssp[:, 4:8], op=ALU.add)
+            ssp = small.tile([P, 4], F32, name="ssp%d" % s, tag="ssp")
+            for u in range(2):
+                for e in range(2):
+                    t = 2 * u + e
+                    nc.scalar.activation(
+                        out=junk[:], in_=r16(s, u)[:, :, e], func=ACT.Square,
+                        accum_out=ssp[:, t:t + 1],
+                    )
             ssc = small.tile([P, 4], F32, name="ssc%d" % s, tag="ssc")
-            nc.vector.tensor_scalar_max(out=ssc[:], in0=ss[:], scalar1=TINY)
-            st[("ssc", s)] = ssc
-
-        def do_pow(s):
-            if not ok(s):
-                return
+            nc.gpsimd.tensor_scalar(out=ssc[:], in0=ssp[:], scalar1=TINY, scalar2=None, op0=ALU.max)
             rn = small.tile([P, 4], F32, name="rn%d" % s, tag="rn")
-            nc.gpsimd.tensor_tensor(out=rn[:], in0=st[("ssc", s)][:], in1=neghalf[:], op=ALU.pow)
+            nc.gpsimd.tensor_tensor(out=rn[:], in0=ssc[:], in1=expo_a[:], op=ALU.pow)
             st[("rn", s)] = rn
 
+        def do_n2u(s):
+            rn = st[("rn", s)]
+            xu = big.tile([P, 2048], BF16, name="xu%d" % s, tag="xu")
+            for u in range(2):
+                for e in range(2):
+                    t = 2 * u + e
+                    nc.scalar.activation(
+                        out=xu[:, t * 512:(t + 1) * 512], in_=r16(s, u)[:, :, e], func=ACT.Copy,
+                        scale=rn[:, t:t + 1],
+                    )
+            st[("xu", s)] = xu
+
         def do_b(s):
-            if not ok(s):
-                return
             rn = st[("rn", s)]
             bt = ps_b.tile([P, 512], F32, name="bt%d" % s, tag="B")
             for t in range(4):
@@ -154,23 +147,15 @@ def tile_netvlad_kernel(tc, x, conv_w, conv_b, centroids, out):
                 )
             st[("B", s)] = bt
 
-        def do_n2(s):
-            if not ok(s):
-                return
-            rn = st[("rn", s)]
+        def do_regroup(s):
             xg = big.tile([P, 2048], BF16, name="xg%d" % s, tag="xg", align_bytes=64)
-            xg4 = xg[:].rearrange("p (c u e) -> p c u e", u=2, e=2)
-            rn4 = rn[:].rearrange("p (u e) -> p u e", u=2).unsqueeze(1).to_broadcast([P, 256, 2, 2])
-            for h in range(2):
-                r16 = st[("R", s)][h][:].bitcast(BF16).rearrange("p (u c e) -> p c u e", u=2, e=2)
-                nc.vector.tensor_tensor(
-                    out=xg4[:, 256 * h:256 * (h + 1)], in0=r16, in1=rn4, op=ALU.mult
-                )
+            nc.vector.tensor_copy(
+                out=xg[:].rearrange("p (c i t) -> p c t i", i=4, t=4),
+                in_=st[("xu", s)][:].rearrange("p (t c i) -> p c t i", t=4, i=4),
+            )
             st[("xg", s)] = xg
 
         def do_n1(s):
-            if not ok(s):
-                return
             n, g = divmod(s, 2)
             cg = big.tile([P, 2048], BF16, name="cg%d" % s, tag="cg", align_bytes=64)
             cg4 = cg[:].rearrange("p (t q j) -> p t q j", t=4, j=4)
@@ -186,24 +171,18 @@ def tile_netvlad_kernel(tc, x, conv_w, conv_b, centroids, out):
             st[("cg", s)] = cg
 
         def do_qp(s):
-            if not ok(s):
-                return
             xpc = keep.tile([P, 512], U32, name="xpc%d" % s, tag="xpc", align_bytes=64)
             xps = keep.tile([P, 512], U8, name="xps%d" % s, tag="xps", align_bytes=64)
             nc.vector.quantize_mx(out=xpc[:].bitcast(FP8X4), scales=xps[:], in_=st[("xg", s)][:])
             st[("xp", s)] = (xpc, xps)
 
         def do_qc(s):
-            if not ok(s):
-                return
-            xcc = big.tile([P, 512], U32, name="xcc%d" % s, tag="xcc", align_bytes=64)
-            xcs = big.tile([P, 512], U8, name="xcs%d" % s, tag="xcs", align_bytes=64)
+            xcc = soft.tile([P, 512], U32, name="xcc%d" % s, tag="xcc", align_bytes=64)
+            xcs = soft.tile([P, 512], U8, name="xcs%d" % s, tag="xcs", align_bytes=64)
             nc.vector.quantize_mx(out=xcc[:].bitcast(FP8X4), scales=xcs[:], in_=st[("cg", s)][:])
             st[("xc", s)] = (xcc, xcs)
 
         def do_mx1(s):
-            if not ok(s):
-                return
             xcc, xcs = st[("xc", s)]
             lt = ps_l.tile([P, 512], F32, name="lt%d" % s, tag="L")
             for t in range(4):
@@ -216,68 +195,64 @@ def tile_netvlad_kernel(tc, x, conv_w, conv_b, centroids, out):
                 )
             st[("L", s)] = lt
 
-        def do_addmax(s):
-            if not ok(s):
-                return
+        def do_add(s):
             z = soft.tile([P, 512], F32, name="z%d" % s, tag="z")
-            z3 = z[:].rearrange("p (t k) -> p t k", t=4)
             nc.vector.tensor_tensor(
-                out=z3, in0=st[("L", s)][:].rearrange("p (t k) -> p t k", t=4),
+                out=z[:].rearrange("p (t k) -> p t k", t=4),
+                in0=st[("L", s)][:].rearrange("p (t k) -> p t k", t=4),
                 in1=b_bc[:].unsqueeze(1).to_broadcast([P, 4, 128]), op=ALU.add,
             )
-            negm = small.tile([P, 4], F32, name="negm%d" % s, tag="negm")
-            nc.vector.tensor_reduce(out=negm[:], in_=z3, axis=AX.X, op=ALU.max, negate=True)
-            st[("z", s)] = (z, negm)
+            st[("z", s)] = z
 
-        def do_exp(s):
-            if not ok(s):
-                return
-            z, negm = st[("z", s)]
+        def do_max(s):
+            negm = small.tile([P, 4], F32, name="negm%d" % s, tag="negm")
+            nc.vector.tensor_reduce(
+                out=negm[:], in_=st[("z", s)][:].rearrange("p (t k) -> p t k", t=4),
+                axis=AX.X, op=ALU.max, negate=True,
+            )
+            st[("negm", s)] = negm
+
+        def do_exp(s, cb):
+            z = st[("z", s)]
+            negm = st[("negm", s)]
             ex = soft.tile([P, 512], F32, name="ex%d" % s, tag="ex")
-            sums = small.tile([P, 4], F32, name="sums%d" % s, tag="sums")
             for t in range(4):
                 cols = slice(t * 128, (t + 1) * 128)
                 nc.scalar.activation(
                     out=ex[:, cols], in_=z[:, cols], func=ACT.Exp,
-                    bias=negm[:, t:t + 1], scale=1.0, accum_out=sums[:, t:t + 1],
+                    bias=negm[:, t:t + 1], scale=1.0, accum_out=cb[:, t:t + 1],
                 )
-            st[("ex", s)] = (ex, sums)
+            st[("ex", s)] = ex
 
-        def do_a(s):
-            if not ok(s):
-                return
-            ex, sums = st[("ex", s)]
-            rs = small.tile([P, 4], F32, name="rs%d" % s, tag="rs")
-            nc.vector.reciprocal(out=rs[:], in_=sums[:])
-            ag = big.tile([P, 512], BF16, name="ag%d" % s, tag="ag", align_bytes=64)
-            nc.vector.tensor_tensor(
-                out=ag[:].rearrange("p (k t) -> p k t", t=4),
-                in0=ex[:].rearrange("p (t k) -> p k t", t=4),
-                in1=rs[:].unsqueeze(1).to_broadcast([P, 128, 4]), op=ALU.mult,
-            )
-            st[("rs", s)] = rs
-            st[("ag", s)] = ag
-
-        def do_qa(s):
-            if not ok(s):
-                return
-            ac = big.tile([P, 128], U32, name="ac%d" % s, tag="ac", align_bytes=64)
-            asc = big.tile([P, 128], U8, name="asc%d" % s, tag="asc", align_bytes=64)
-            nc.vector.quantize_mx(out=ac[:].bitcast(FP8X4), scales=asc[:], in_=st[("ag", s)][:])
-            st[("a", s)] = (ac, asc)
-
-        def do_mx2(s):
-            if not ok(s):
-                return
+        def do_asum(s):
             n, g = divmod(s, 2)
-            ex, sums = st[("ex", s)]
-            rs = st[("rs", s)]
+            ex = st[("ex", s)]
+            rs = st[("res", s + 1)]
             col = 4 * (n % 2) + g
             for t in range(4):
                 nc.tensor.matmul(
                     out=misc[:, col:col + 1], lhsT=ex[:, t * 128:(t + 1) * 128],
                     rhs=rs[:, t:t + 1], start=(t == 0), stop=(t == 3),
                 )
+
+        def do_ag(s):
+            rs = st[("res", s + 1)]
+            ag = big.tile([P, 512], BF16, name="ag%d" % s, tag="ag", align_bytes=64)
+            nc.vector.tensor_tensor(
+                out=ag[:].rearrange("p (k t) -> p k t", t=4),
+                in0=st[("ex", s)][:].rearrange("p (t k) -> p k t", t=4),
+                in1=rs[:, 0:4].unsqueeze(1).to_broadcast([P, 128, 4]), op=ALU.mult,
+            )
+            st[("ag", s)] = ag
+
+        def do_qa(s):
+            ac = big.tile([P, 128], U32, name="ac%d" % s, tag="ac", align_bytes=64)
+            asc = big.tile([P, 128], U8, name="asc%d" % s, tag="asc", align_bytes=64)
+            nc.vector.quantize_mx(out=ac[:].bitcast(FP8X4), scales=asc[:], in_=st[("ag", s)][:])
+            st[("a", s)] = (ac, asc)
+
+        def do_mx2(s):
+            n, g = divmod(s, 2)
             if g == 0:
                 st[("V", n)] = ps_v.tile([P, 512], F32, name="vl%d" % n, tag="V")
             ac, asc = st[("a", s)]
@@ -289,15 +264,12 @@ def tile_netvlad_kernel(tc, x, conv_w, conv_b, centroids, out):
                 start=(g == 0), stop=(g == 1),
             )
 
-        def img(num):
-            if num % 2 == 0 and 0 <= num // 2 < N_IMG:
-                return num // 2
-            return None
-
-        def fin_a(n):
+        def fin_a(n, cb):
             c0 = 4 * (n % 2)
             nas = small.tile([P, 1], F32, name="nas%d" % n, tag="nas")
-            nc.vector.tensor_reduce(out=nas[:], in_=misc[:, c0:c0 + 2], axis=AX.X, op=ALU.add, negate=True)
+            nc.scalar.activation(
+                out=junk3[:], in_=misc[:, c0:c0 + 2], func=ACT.Copy, scale=-1.0, accum_out=nas[:]
+            )
             vv = soft.tile([P, C], F32, name="vv%d" % n, tag="vv")
             nc.vector.scalar_tensor_tensor(
                 out=vv[:].rearrange("p (q j) -> p q j", j=4),
@@ -306,78 +278,85 @@ def tile_netvlad_kernel(tc, x, conv_w, conv_b, centroids, out):
                 in1=st[("V", n)][:].rearrange("p (j q) -> p q j", j=4),
                 op0=ALU.mult, op1=ALU.add,
             )
-            ssr = small.tile([P, 1], F32, name="ssr%d" % n, tag="ssr")
-            nc.scalar.activation(out=junk2[:], in_=vv[:], func=ACT.Square, accum_out=ssr[:])
+            nc.scalar.activation(out=junk[:], in_=vv[:], func=ACT.Square, accum_out=cb[:, 4:5])
             st[("vv", n)] = vv
-            st[("ssr", n)] = ssr
+            st[("ssr", n)] = cb
 
-        def fin_clamp_r(n):
-            src = small.tile([P, 1], F32, name="src%d" % n, tag="src")
-            nc.vector.tensor_scalar_max(out=src[:], in0=st[("ssr", n)][:], scalar1=TINY)
-            st[("src", n)] = src
-
-        def fin_pow_r(n):
-            rk = small.tile([P, 1], F32, name="rk%d" % n, tag="rk")
-            nc.gpsimd.tensor_tensor(out=rk[:], in0=st[("src", n)][:], in1=neghalf[:, 0:1], op=ALU.pow)
-            st[("rk", n)] = rk
-
-        def fin_gsum(n):
-            rk = st[("rk", n)]
+        def fin_b(n, p, cb):
+            rk = st[("res", p - 1)]
             val = small.tile([P, 1], F32, name="val%d" % n, tag="val")
             nc.vector.scalar_tensor_tensor(
-                out=val[:], in0=st[("ssr", n)][:], scalar=rk[:, 0:1], in1=rk[:],
+                out=val[:], in0=st[("ssr", n)][:, 4:5], scalar=rk[:, 4:5], in1=rk[:, 4:5],
                 op0=ALU.mult, op1=ALU.mult,
             )
             c0 = 4 * (n % 2) + 2
             nc.tensor.matmul(out=misc[:, c0:c0 + 1], lhsT=onesm[:], rhs=val[:], start=True, stop=True)
+            nc.scalar.activation(out=cb[:, 4:5], in_=misc[:, c0:c0 + 1], func=ACT.Copy)
 
-        def fin_clamp_g(n):
-            c0 = 4 * (n % 2) + 2
-            gs = small.tile([P, 1], F32, name="gs%d" % n, tag="gs")
-            nc.vector.tensor_scalar_max(out=gs[:], in0=misc[:, c0:c0 + 1], scalar1=TINY)
-            st[("gs", n)] = gs
-
-        def fin_out(n):
-            rg = small.tile([P, 1], F32, name="rg%d" % n, tag="rg")
-            nc.gpsimd.tensor_tensor(out=rg[:], in0=st[("gs", n)][:], in1=neghalf[:, 0:1], op=ALU.pow)
+        def fin_c(n, p):
+            rk = st[("res", p - 2)]
+            rg = st[("res", p - 1)]
             ot = soft.tile([P, C], F32, name="ot%d" % n, tag="ot")
             nc.gpsimd.tensor_scalar(
-                out=ot[:], in0=st[("vv", n)][:], scalar1=st[("rk", n)][:, 0:1], scalar2=rg[:, 0:1],
+                out=ot[:], in0=st[("vv", n)][:], scalar1=rk[:, 4:5], scalar2=rg[:, 4:5],
                 op0=ALU.mult, op1=ALU.mult,
             )
             o2 = out[n].rearrange("(k c) -> k c", c=C)
             nc.sync.dma_start(out=o2[0:112, :], in_=ot[0:112, :])
             nc.sync.dma_start(out=o2[112:127, :], in_=ot[112:127, :])
 
-        for s in range(-2, NU + 4):
-            na = img(s - 4)
-            nb = img(s - 5)
+        for p in range(-2, NU + 5):
+            na = img(p - 4)
+            nb = img(p - 5)
+            ncc = img(p - 6)
+            if ok(p - 3):
+                do_qa(p - 3)
+            if ok(p - 1):
+                do_mx1(p - 1)
+            if ok(p - 3):
+                do_mx2(p - 3)
+            if ok(p + 2):
+                do_t(p + 2)
+            if ok(p + 1):
+                do_n2u(p + 1)
+            if ok(p + 2):
+                do_ss(p + 2)
+            if ok(p):
+                do_regroup(p)
+                do_n1(p)
+                if p % 2 == 1:
+                    load(p // 2 + 4)
+                do_qp(p)
+            if ok(p - 1):
+                do_add(p - 1)
+            if ok(p):
+                do_qc(p)
+            lo = 0 if ok(p - 1) else 4
+            hi = 5 if (na is not None or nb is not None) else 4
+            cb = None
+            if hi > lo:
+                cb = small.tile([P, 5], F32, name="cb%d" % p, tag="cb")
+            if ok(p - 1):
+                do_max(p - 1)
+                do_exp(p - 1, cb)
+            if ok(p - 2):
+                do_asum(p - 2)
+                do_ag(p - 2)
             if na is not None:
-                fin_a(na)
-            do_n2(s)
-            do_t(s + 2)
-            do_ss(s + 2)
-            do_n1(s)
-            if s >= 0 and s % 2 == 1:
-                load(s // 2 + 4)
-            do_ssadd(s + 1)
-            if na is not None:
-                fin_clamp_r(na)
+                fin_a(na, cb)
             if nb is not None:
-                fin_clamp_g(nb)
-            do_pow(s + 1)
-            if na is not None:
-                fin_pow_r(na)
-            if nb is not None:
-                fin_out(nb)
-            do_b(s + 1)
-            do_qp(s)
-            do_addmax(s - 1)
-            do_exp(s - 1)
-            if na is not None:
-                fin_gsum(na)
-            do_qc(s)
-            do_mx1(s)
-            do_a(s - 2)
-            do_qa(s - 2)
-            do_mx2(s - 2)
+                fin_b(nb, p, cb)
+            if ok(p + 1):
+                do_b(p + 1)
+            if ncc is not None:
+                fin_c(ncc, p)
+            if hi > lo:
+                cbc = small.tile([P, 5], F32, name="cbc%d" % p, tag="cbc")
+                nc.gpsimd.tensor_scalar(
+                    out=cbc[:, lo:hi], in0=cb[:, lo:hi], scalar1=TINY, scalar2=None, op0=ALU.max
+                )
+                res = small.tile([P, 5], F32, name="res%d" % p, tag="res")
+                nc.gpsimd.tensor_tensor(
+                    out=res[:, lo:hi], in0=cbc[:, lo:hi], in1=expo_b[:, lo:hi], op=ALU.pow
+                )
+                st[("res", p)] = res

@@ -27,7 +27,7 @@ def tile_netvlad_kernel(tc, x, conv_w, conv_b, centroids, out):
         const = ctx.enter_context(tc.tile_pool(name="const", bufs=1))
         xpool = ctx.enter_context(tc.tile_pool(name="xpool", bufs=4))
         big = ctx.enter_context(tc.tile_pool(name="big", bufs=2))
-        keep = ctx.enter_context(tc.tile_pool(name="keep", bufs=5))
+        keep = ctx.enter_context(tc.tile_pool(name="keep", bufs=4))
         soft = ctx.enter_context(tc.tile_pool(name="soft", bufs=3))
         small = ctx.enter_context(tc.tile_pool(name="small", bufs=6))
         ps_r = ctx.enter_context(tc.psum_pool(name="ps_r", bufs=4))
@@ -39,16 +39,22 @@ def tile_netvlad_kernel(tc, x, conv_w, conv_b, centroids, out):
 
         xs = {}
 
-        def load(n):
+        def load(n, halves=False):
             if n >= N_IMG:
                 return
             xt = xpool.tile([P, 4 * PX], BF16, name="xt%d" % n, tag="xt")
-            nc.sync.dma_start(out=xt[:], in_=x[n].rearrange("(q j) h w -> q (j h w)", j=4))
+            if halves:
+                src = x[n].rearrange("(q j) h w -> q j (h w)", j=4)
+                dst = xt[:].rearrange("p (j w) -> p j w", j=4)
+                for g in range(2):
+                    nc.sync.dma_start(out=dst[:, :, 512 * g:512 * (g + 1)], in_=src[:, :, 512 * g:512 * (g + 1)])
+            else:
+                nc.sync.dma_start(out=xt[:], in_=x[n].rearrange("(q j) h w -> q (j h w)", j=4))
             xs[n] = xt
 
         w_sb = const.tile([P, C], BF16, name="w_sb")
         nc.sync.dma_start(out=w_sb[:], in_=conv_w)
-        load(0)
+        load(0, halves=True)
         b_bc = const.tile([P, 128], BF16, name="b_bc")
         nc.sync.dma_start(out=b_bc[:], in_=conv_b.partition_broadcast(P))
         cent = const.tile([P, C], BF16, name="cent")
@@ -148,17 +154,16 @@ def tile_netvlad_kernel(tc, x, conv_w, conv_b, centroids, out):
             st[("B", s)] = bt
 
         def do_regroup(s):
-            xg = big.tile([P, 2048], BF16, name="xg%d" % s, tag="xg", align_bytes=64)
             nc.vector.tensor_copy(
-                out=xg[:].rearrange("p (c i t) -> p c t i", i=4, t=4),
+                out=st[("qin", s)][:, 2048:4096].rearrange("p (c i t) -> p c t i", i=4, t=4),
                 in_=st[("xu", s)][:].rearrange("p (t c i) -> p c t i", t=4, i=4),
             )
-            st[("xg", s)] = xg
 
         def do_n1(s):
             n, g = divmod(s, 2)
-            cg = big.tile([P, 2048], BF16, name="cg%d" % s, tag="cg", align_bytes=64)
-            cg4 = cg[:].rearrange("p (t q j) -> p t q j", t=4, j=4)
+            qin = big.tile([P, 4096], BF16, name="qin%d" % s, tag="qin", align_bytes=64)
+            st[("qin", s)] = qin
+            cg4 = qin[:, 0:2048].rearrange("p (t q j) -> p t q j", t=4, j=4)
             xv = xs[n][:].rearrange("p (j g u q e) -> p g u e q j", j=4, g=2, u=2, e=2)
             b3 = st[("B", s)][:].rearrange("p (t q) -> p t q", t=4)
             for u in range(2):
@@ -168,22 +173,15 @@ def tile_netvlad_kernel(tc, x, conv_w, conv_b, centroids, out):
                     in1=b3[:, 2 * u:2 * u + 2, :].unsqueeze(3).to_broadcast([P, 2, 128, 4]),
                     op=ALU.mult,
                 )
-            st[("cg", s)] = cg
 
-        def do_qp(s):
-            xpc = keep.tile([P, 512], U32, name="xpc%d" % s, tag="xpc", align_bytes=64)
-            xps = keep.tile([P, 512], U8, name="xps%d" % s, tag="xps", align_bytes=64)
-            nc.vector.quantize_mx(out=xpc[:].bitcast(FP8X4), scales=xps[:], in_=st[("xg", s)][:])
-            st[("xp", s)] = (xpc, xps)
-
-        def do_qc(s):
-            xcc = soft.tile([P, 512], U32, name="xcc%d" % s, tag="xcc", align_bytes=64)
-            xcs = soft.tile([P, 512], U8, name="xcs%d" % s, tag="xcs", align_bytes=64)
-            nc.vector.quantize_mx(out=xcc[:].bitcast(FP8X4), scales=xcs[:], in_=st[("cg", s)][:])
-            st[("xc", s)] = (xcc, xcs)
+        def do_q(s):
+            qc = keep.tile([P, 1024], U32, name="qc%d" % s, tag="qc", align_bytes=64)
+            qs = keep.tile([P, 1024], U8, name="qs%d" % s, tag="qs", align_bytes=64)
+            nc.vector.quantize_mx(out=qc[:].bitcast(FP8X4), scales=qs[:], in_=st[("qin", s)][:])
+            st[("q", s)] = (qc, qs)
 
         def do_mx1(s):
-            xcc, xcs = st[("xc", s)]
+            xcc, xcs = st[("q", s)]
             lt = ps_l.tile([P, 512], F32, name="lt%d" % s, tag="L")
             for t in range(4):
                 cols = slice(t * 128, (t + 1) * 128)
@@ -238,7 +236,7 @@ def tile_netvlad_kernel(tc, x, conv_w, conv_b, centroids, out):
         def do_ag(s):
             rs = st[("res", s + 1)]
             ag = big.tile([P, 512], BF16, name="ag%d" % s, tag="ag", align_bytes=64)
-            nc.vector.tensor_tensor(
+            nc.gpsimd.tensor_tensor(
                 out=ag[:].rearrange("p (k t) -> p k t", t=4),
                 in0=st[("ex", s)][:].rearrange("p (t k) -> p k t", t=4),
                 in1=rs[:, 0:4].unsqueeze(1).to_broadcast([P, 128, 4]), op=ALU.mult,
@@ -256,20 +254,24 @@ def tile_netvlad_kernel(tc, x, conv_w, conv_b, centroids, out):
             if g == 0:
                 st[("V", n)] = ps_v.tile([P, 512], F32, name="vl%d" % n, tag="V")
             ac, asc = st[("a", s)]
-            xpc, xps = st[("xp", s)]
+            qc, qs = st[("q", s)]
             nc.tensor.matmul_mx(
                 out=st[("V", n)][:],
                 lhsT=ac[:].bitcast(FP8X4), lhsT_scale=asc[:],
-                rhs=xpc[:].bitcast(FP8X4), rhs_scale=xps[:],
+                rhs=qc[:, 512:1024].bitcast(FP8X4), rhs_scale=qs[:, 512:1024],
                 start=(g == 0), stop=(g == 1),
             )
 
-        def fin_a(n, cb):
+        def fin_nas(n):
             c0 = 4 * (n % 2)
             nas = small.tile([P, 1], F32, name="nas%d" % n, tag="nas")
             nc.scalar.activation(
                 out=junk3[:], in_=misc[:, c0:c0 + 2], func=ACT.Copy, scale=-1.0, accum_out=nas[:]
             )
+            st[("nas", n)] = nas
+
+        def fin_stt(n):
+            nas = st[("nas", n)]
             vv = soft.tile([P, C], F32, name="vv%d" % n, tag="vv")
             nc.vector.scalar_tensor_tensor(
                 out=vv[:].rearrange("p (q j) -> p q j", j=4),
@@ -278,8 +280,10 @@ def tile_netvlad_kernel(tc, x, conv_w, conv_b, centroids, out):
                 in1=st[("V", n)][:].rearrange("p (j q) -> p q j", j=4),
                 op0=ALU.mult, op1=ALU.add,
             )
-            nc.scalar.activation(out=junk[:], in_=vv[:], func=ACT.Square, accum_out=cb[:, 4:5])
             st[("vv", n)] = vv
+
+        def fin_sq(n, cb):
+            nc.scalar.activation(out=junk[:], in_=st[("vv", n)][:], func=ACT.Square, accum_out=cb[:, 4:5])
             st[("ssr", n)] = cb
 
         def fin_b(n, p, cb):
@@ -309,28 +313,27 @@ def tile_netvlad_kernel(tc, x, conv_w, conv_b, centroids, out):
             na = img(p - 4)
             nb = img(p - 5)
             ncc = img(p - 6)
-            if ok(p - 3):
-                do_qa(p - 3)
             if ok(p - 1):
                 do_mx1(p - 1)
-            if ok(p - 3):
-                do_mx2(p - 3)
             if ok(p + 2):
                 do_t(p + 2)
+            if na is not None:
+                fin_nas(na)
             if ok(p + 1):
                 do_n2u(p + 1)
             if ok(p + 2):
                 do_ss(p + 2)
             if ok(p):
-                do_regroup(p)
                 do_n1(p)
                 if p % 2 == 1:
                     load(p // 2 + 4)
-                do_qp(p)
+                do_regroup(p)
             if ok(p - 1):
                 do_add(p - 1)
+            if na is not None:
+                fin_stt(na)
             if ok(p):
-                do_qc(p)
+                do_q(p)
             lo = 0 if ok(p - 1) else 4
             hi = 5 if (na is not None or nb is not None) else 4
             cb = None
@@ -341,13 +344,15 @@ def tile_netvlad_kernel(tc, x, conv_w, conv_b, centroids, out):
                 do_exp(p - 1, cb)
             if ok(p - 2):
                 do_asum(p - 2)
-                do_ag(p - 2)
+                do_qa(p - 2)
             if na is not None:
-                fin_a(na, cb)
+                fin_sq(na, cb)
             if nb is not None:
                 fin_b(nb, p, cb)
             if ok(p + 1):
                 do_b(p + 1)
+            if ok(p - 2):
+                do_mx2(p - 2)
             if ncc is not None:
                 fin_c(ncc, p)
             if hi > lo:
@@ -360,3 +365,5 @@ def tile_netvlad_kernel(tc, x, conv_w, conv_b, centroids, out):
                     out=res[:, lo:hi], in0=cbc[:, lo:hi], in1=expo_b[:, lo:hi], op=ALU.pow
                 )
                 st[("res", p)] = res
+            if ok(p - 1):
+                do_ag(p - 1)

@@ -319,15 +319,19 @@ def tile_netvlad_kernel(tc, x, conv_w, conv_b, centroids, out):
                 do_t(p + 2)
             if na is not None:
                 fin_nas(na)
+            if p < 0 and ok(p + 2):
+                do_ss(p + 2)
             if ok(p + 1):
                 do_n2u(p + 1)
-            if ok(p + 2):
+            if p >= 0 and ok(p + 2):
                 do_ss(p + 2)
             if ok(p):
                 do_n1(p)
                 if p % 2 == 1:
                     load(p // 2 + 4)
                 do_regroup(p)
+            if ok(p + 1):
+                do_b(p + 1)
             if ok(p - 1):
                 do_add(p - 1)
             if na is not None:
@@ -345,16 +349,12 @@ def tile_netvlad_kernel(tc, x, conv_w, conv_b, centroids, out):
             if ok(p - 2):
                 do_asum(p - 2)
                 do_qa(p - 2)
-            if na is not None:
-                fin_sq(na, cb)
             if nb is not None:
                 fin_b(nb, p, cb)
-            if ok(p + 1):
-                do_b(p + 1)
+            if na is not None:
+                fin_sq(na, cb)
             if ok(p - 2):
                 do_mx2(p - 2)
-            if ncc is not None:
-                fin_c(ncc, p)
             if hi > lo:
                 cbc = small.tile([P, 5], F32, name="cbc%d" % p, tag="cbc")
                 nc.gpsimd.tensor_scalar(
@@ -367,3 +367,5 @@ def tile_netvlad_kernel(tc, x, conv_w, conv_b, centroids, out):
                 st[("res", p)] = res
             if ok(p - 1):
                 do_ag(p - 1)
+            if ncc is not None:
+                fin_c(ncc, p)

@@ -65,11 +65,8 @@ def tile_netvlad_kernel(tc, x, conv_w, conv_b, centroids, out):
 
         ident = const.tile([P, P], F32, name="ident")
         make_identity(nc, ident[:])
-        expo_a = const.tile([P, 4], F32, name="expo_a")
-        nc.gpsimd.memset(expo_a[:], -0.5)
-        expo_b = const.tile([P, 5], F32, name="expo_b")
-        nc.gpsimd.memset(expo_b[:, 0:4], -1.0)
-        nc.gpsimd.memset(expo_b[:, 4:5], -0.5)
+        expo = const.tile([P, 6], F32, name="expo")
+        nc.gpsimd.memset(expo[:], -0.5)
         onesm = const.tile([P, P], F32, name="onesm")
         nc.vector.tensor_scalar(
             out=onesm[:], in0=ident[:, 127:128].to_broadcast([P, P]),
@@ -117,23 +114,32 @@ def tile_netvlad_kernel(tc, x, conv_w, conv_b, centroids, out):
                 banks.append(ru)
             st[("R", s)] = banks
 
-        def do_ss(s):
-            ssp = small.tile([P, 4], F32, name="ssp%d" % s, tag="ssp")
+        def comb(p):
+            if ("cb", p) not in st:
+                st[("cb", p)] = small.tile([P, 6], F32, name="cb%d" % p, tag="cb")
+            return st[("cb", p)]
+
+        def do_ss(s, cb):
             for u in range(2):
                 for e in range(2):
                     t = 2 * u + e
                     nc.scalar.activation(
                         out=junk[:], in_=r16(s, u)[:, :, e], func=ACT.Square,
-                        accum_out=ssp[:, t:t + 1],
+                        accum_out=cb[:, t:t + 1],
                     )
-            ssc = small.tile([P, 4], F32, name="ssc%d" % s, tag="ssc")
-            nc.gpsimd.tensor_scalar(out=ssc[:], in0=ssp[:], scalar1=TINY, scalar2=None, op0=ALU.max)
-            rn = small.tile([P, 4], F32, name="rn%d" % s, tag="rn")
-            nc.gpsimd.tensor_tensor(out=rn[:], in0=ssc[:], in1=expo_a[:], op=ALU.pow)
-            st[("rn", s)] = rn
+
+        def do_pow(p, lo, hi):
+            cb = st[("cb", p)]
+            cbc = small.tile([P, 6], F32, name="cbc%d" % p, tag="cbc")
+            nc.gpsimd.tensor_scalar(
+                out=cbc[:, lo:hi], in0=cb[:, lo:hi], scalar1=TINY, scalar2=None, op0=ALU.max
+            )
+            res = small.tile([P, 6], F32, name="res%d" % p, tag="res")
+            nc.gpsimd.tensor_tensor(out=res[:, lo:hi], in0=cbc[:, lo:hi], in1=expo[:, lo:hi], op=ALU.pow)
+            st[("res", p)] = res
 
         def do_n2u(s):
-            rn = st[("rn", s)]
+            rn = st[("res", s - 2)]
             xu = big.tile([P, 2048], BF16, name="xu%d" % s, tag="xu")
             for u in range(2):
                 for e in range(2):
@@ -145,7 +151,7 @@ def tile_netvlad_kernel(tc, x, conv_w, conv_b, centroids, out):
             st[("xu", s)] = xu
 
         def do_b(s):
-            rn = st[("rn", s)]
+            rn = st[("res", s - 2)]
             bt = ps_b.tile([P, 512], F32, name="bt%d" % s, tag="B")
             for t in range(4):
                 nc.tensor.transpose(
@@ -210,9 +216,11 @@ def tile_netvlad_kernel(tc, x, conv_w, conv_b, centroids, out):
             )
             st[("negm", s)] = negm
 
-        def do_exp(s, cb):
+        def do_exp(s):
             z = st[("z", s)]
             negm = st[("negm", s)]
+            cb = small.tile([P, 4], F32, name="sums%d" % s, tag="sums")
+            st[("sums", s)] = cb
             ex = soft.tile([P, 512], F32, name="ex%d" % s, tag="ex")
             for t in range(4):
                 cols = slice(t * 128, (t + 1) * 128)
@@ -222,10 +230,15 @@ def tile_netvlad_kernel(tc, x, conv_w, conv_b, centroids, out):
                 )
             st[("ex", s)] = ex
 
+        def do_recip(s):
+            rs = small.tile([P, 4], F32, name="rs%d" % s, tag="rs")
+            nc.vector.reciprocal(out=rs[:], in_=st[("sums", s)][:])
+            st[("rs", s)] = rs
+
         def do_asum(s):
             n, g = divmod(s, 2)
             ex = st[("ex", s)]
-            rs = st[("res", s + 1)]
+            rs = st[("rs", s)]
             col = 4 * (n % 2) + g
             for t in range(4):
                 nc.tensor.matmul(
@@ -234,7 +247,7 @@ def tile_netvlad_kernel(tc, x, conv_w, conv_b, centroids, out):
                 )
 
         def do_ag(s):
-            rs = st[("res", s + 1)]
+            rs = st[("rs", s)]
             ag = big.tile([P, 512], BF16, name="ag%d" % s, tag="ag", align_bytes=64)
             nc.gpsimd.tensor_tensor(
                 out=ag[:].rearrange("p (k t) -> p k t", t=4),
@@ -295,77 +308,75 @@ def tile_netvlad_kernel(tc, x, conv_w, conv_b, centroids, out):
             )
             c0 = 4 * (n % 2) + 2
             nc.tensor.matmul(out=misc[:, c0:c0 + 1], lhsT=onesm[:], rhs=val[:], start=True, stop=True)
-            nc.scalar.activation(out=cb[:, 4:5], in_=misc[:, c0:c0 + 1], func=ACT.Copy)
+            st[("gcb", n)] = cb
+
+        def fin_gcopy(n):
+            c0 = 4 * (n % 2) + 2
+            nc.scalar.activation(out=st[("gcb", n)][:, 5:6], in_=misc[:, c0:c0 + 1], func=ACT.Copy)
 
         def fin_c(n, p):
-            rk = st[("res", p - 2)]
+            rk = st[("res", p - 3)]
             rg = st[("res", p - 1)]
             ot = soft.tile([P, C], F32, name="ot%d" % n, tag="ot")
-            nc.gpsimd.tensor_scalar(
-                out=ot[:], in0=st[("vv", n)][:], scalar1=rk[:, 4:5], scalar2=rg[:, 4:5],
+            nc.vector.tensor_scalar(
+                out=ot[:], in0=st[("vv", n)][:], scalar1=rk[:, 4:5], scalar2=rg[:, 5:6],
                 op0=ALU.mult, op1=ALU.mult,
             )
             o2 = out[n].rearrange("(k c) -> k c", c=C)
             nc.sync.dma_start(out=o2[0:112, :], in_=ot[0:112, :])
             nc.sync.dma_start(out=o2[112:127, :], in_=ot[112:127, :])
 
-        for p in range(-2, NU + 5):
+        for p in range(-3, NU + 7):
             na = img(p - 4)
-            nb = img(p - 5)
-            ncc = img(p - 6)
+            nb = img(p - 6)
+            ncc = img(p - 8)
             if ok(p - 1):
                 do_mx1(p - 1)
             if ok(p + 2):
-                do_t(p + 2)
+                do_ss(p + 2, comb(p))
             if na is not None:
                 fin_nas(na)
-            if p < 0 and ok(p + 2):
-                do_ss(p + 2)
-            if ok(p + 1):
-                do_n2u(p + 1)
-            if p >= 0 and ok(p + 2):
-                do_ss(p + 2)
             if ok(p):
                 do_n1(p)
                 if p % 2 == 1:
                     load(p // 2 + 4)
+            if ok(p - 2):
+                do_recip(p - 2)
+                do_ag(p - 2)
+            has_r = img(p - 5) is not None
+            has_g = img(p - 7) is not None
+            lo = 0 if ok(p + 2) else (4 if has_r else 5)
+            hi = 6 if has_g else (5 if has_r else 4)
+            if hi > lo:
+                do_pow(p, lo, hi)
+            if ok(p + 1):
+                do_n2u(p + 1)
+            if ok(p):
                 do_regroup(p)
             if ok(p + 1):
                 do_b(p + 1)
             if ok(p - 1):
                 do_add(p - 1)
-            if na is not None:
-                fin_stt(na)
-            if ok(p):
-                do_q(p)
-            lo = 0 if ok(p - 1) else 4
-            hi = 5 if (na is not None or nb is not None) else 4
-            cb = None
-            if hi > lo:
-                cb = small.tile([P, 5], F32, name="cb%d" % p, tag="cb")
-            if ok(p - 1):
-                do_max(p - 1)
-                do_exp(p - 1, cb)
             if ok(p - 2):
                 do_asum(p - 2)
-                do_qa(p - 2)
-            if nb is not None:
-                fin_b(nb, p, cb)
             if na is not None:
-                fin_sq(na, cb)
-            if ok(p - 2):
-                do_mx2(p - 2)
-            if hi > lo:
-                cbc = small.tile([P, 5], F32, name="cbc%d" % p, tag="cbc")
-                nc.gpsimd.tensor_scalar(
-                    out=cbc[:, lo:hi], in0=cb[:, lo:hi], scalar1=TINY, scalar2=None, op0=ALU.max
-                )
-                res = small.tile([P, 5], F32, name="res%d" % p, tag="res")
-                nc.gpsimd.tensor_tensor(
-                    out=res[:, lo:hi], in0=cbc[:, lo:hi], in1=expo_b[:, lo:hi], op=ALU.pow
-                )
-                st[("res", p)] = res
-            if ok(p - 1):
-                do_ag(p - 1)
+                fin_stt(na)
             if ncc is not None:
                 fin_c(ncc, p)
+            if ok(p):
+                do_q(p)
+            if ok(p - 1):
+                do_max(p - 1)
+                do_exp(p - 1)
+            if nb is not None:
+                fin_b(nb, p, comb(p + 1))
+            if ok(p + 3):
+                do_t(p + 3)
+            if ok(p - 2):
+                do_qa(p - 2)
+            if na is not None:
+                fin_sq(na, comb(p + 1))
+            if nb is not None:
+                fin_gcopy(nb)
+            if ok(p - 2):
+                do_mx2(p - 2)

@@ -19,6 +19,7 @@ PX = 1024
 NU = 2 * N_IMG
 TINY = 1e-24
 FLOPS = 2 * 2 * N_IMG * 128 * C * PX
+S_COLS = 64
 
 
 def tile_netvlad_kernel(tc, x, conv_w, conv_b, centroids, out):
@@ -52,9 +53,9 @@ def tile_netvlad_kernel(tc, x, conv_w, conv_b, centroids, out):
                 nc.sync.dma_start(out=xt[:], in_=x[n].rearrange("(q j) h w -> q (j h w)", j=4))
             xs[n] = xt
 
+        load(0, halves=True)
         w_sb = const.tile([P, C], BF16, name="w_sb")
         nc.sync.dma_start(out=w_sb[:], in_=conv_w)
-        load(0, halves=True)
         b_bc = const.tile([P, 128], BF16, name="b_bc")
         nc.sync.dma_start(out=b_bc[:], in_=conv_b.partition_broadcast(P))
         cent = const.tile([P, C], BF16, name="cent")
@@ -76,18 +77,20 @@ def tile_netvlad_kernel(tc, x, conv_w, conv_b, centroids, out):
         junk3 = const.tile([P, 2], F32, name="junk3")
         misc = ps_m.tile([P, 512], F32, name="misc")
 
-        w32 = w_sb[:].bitcast(F32)
-        w_t = ps_r.tile([P, 512], F32, name="w_t", tag="R")
-        for v in range(2):
-            nc.tensor.transpose(w_t[:, v * 128:(v + 1) * 128], w32[:, v:256:2], ident[:])
-        wg = const.tile([P, C], BF16, name="wg", align_bytes=64)
-        nc.vector.tensor_copy(
-            out=wg[:].bitcast(F32).rearrange("p (k v) -> p k v", v=2),
-            in_=w_t[:, 0:256].rearrange("p (v k) -> p k v", v=2),
-        )
         w_codes = const.tile([P, 128], U32, name="w_codes", align_bytes=64)
         w_scales = const.tile([P, 128], U8, name="w_scales", align_bytes=64)
-        nc.vector.quantize_mx(out=w_codes[:].bitcast(FP8X4), scales=w_scales[:], in_=wg[:])
+
+        def setup_w():
+            w32 = w_sb[:].bitcast(F32)
+            w_t = ps_l.tile([P, 512], F32, name="w_t", tag="L")
+            for v in range(2):
+                nc.tensor.transpose(w_t[:, v * 128:(v + 1) * 128], w32[:, v:256:2], ident[:])
+            wg = const.tile([P, C], BF16, name="wg", align_bytes=64)
+            nc.vector.tensor_copy(
+                out=wg[:].bitcast(F32).rearrange("p (k v) -> p k v", v=2),
+                in_=w_t[:, 0:256].rearrange("p (v k) -> p k v", v=2),
+            )
+            nc.vector.quantize_mx(out=w_codes[:].bitcast(FP8X4), scales=w_scales[:], in_=wg[:])
 
         st = {}
 
@@ -159,16 +162,29 @@ def tile_netvlad_kernel(tc, x, conv_w, conv_b, centroids, out):
                 )
             st[("B", s)] = bt
 
+        def qin_of(s):
+            if ("qin", s) not in st:
+                st[("qin", s)] = big.tile([P, 4096], BF16, name="qin%d" % s, tag="qin", align_bytes=64)
+            return st[("qin", s)]
+
+        def regroup_views(s):
+            dst = qin_of(s)[:, 2048:4096].rearrange("p (c i t) -> p c t i", i=4, t=4)
+            src = st[("xu", s)][:].rearrange("p (t c i) -> p c t i", t=4, i=4)
+            return dst, src
+
         def do_regroup(s):
-            nc.vector.tensor_copy(
-                out=st[("qin", s)][:, 2048:4096].rearrange("p (c i t) -> p c t i", i=4, t=4),
-                in_=st[("xu", s)][:].rearrange("p (t c i) -> p c t i", t=4, i=4),
-            )
+            dst, src = regroup_views(s)
+            cut = (C - S_COLS) // 4
+            nc.vector.tensor_copy(out=dst[:, 0:cut], in_=src[:, 0:cut])
+
+        def do_sreg(s):
+            dst, src = regroup_views(s)
+            cut = (C - S_COLS) // 4
+            nc.scalar.copy(out=dst[:, cut:128], in_=src[:, cut:128])
 
         def do_n1(s):
             n, g = divmod(s, 2)
-            qin = big.tile([P, 4096], BF16, name="qin%d" % s, tag="qin", align_bytes=64)
-            st[("qin", s)] = qin
+            qin = qin_of(s)
             cg4 = qin[:, 0:2048].rearrange("p (t q j) -> p t q j", t=4, j=4)
             xv = xs[n][:].rearrange("p (j g u q e) -> p g u e q j", j=4, g=2, u=2, e=2)
             b3 = st[("B", s)][:].rearrange("p (t q) -> p t q", t=4)
@@ -249,7 +265,8 @@ def tile_netvlad_kernel(tc, x, conv_w, conv_b, centroids, out):
         def do_ag(s):
             rs = st[("rs", s)]
             ag = big.tile([P, 512], BF16, name="ag%d" % s, tag="ag", align_bytes=64)
-            nc.gpsimd.tensor_tensor(
+            eng = nc.vector if s >= NU - 2 else nc.gpsimd
+            eng.tensor_tensor(
                 out=ag[:].rearrange("p (k t) -> p k t", t=4),
                 in0=st[("ex", s)][:].rearrange("p (t k) -> p k t", t=4),
                 in1=rs[:, 0:4].unsqueeze(1).to_broadcast([P, 128, 4]), op=ALU.mult,
@@ -297,45 +314,40 @@ def tile_netvlad_kernel(tc, x, conv_w, conv_b, centroids, out):
 
         def fin_sq(n, cb):
             nc.scalar.activation(out=junk[:], in_=st[("vv", n)][:], func=ACT.Square, accum_out=cb[:, 4:5])
-            st[("ssr", n)] = cb
 
-        def fin_b(n, p, cb):
-            rk = st[("res", p - 1)]
+        def fin_b(n, cb):
             val = small.tile([P, 1], F32, name="val%d" % n, tag="val")
-            nc.vector.scalar_tensor_tensor(
-                out=val[:], in0=st[("ssr", n)][:, 4:5], scalar=rk[:, 4:5], in1=rk[:, 4:5],
-                op0=ALU.mult, op1=ALU.mult,
+            nc.vector.tensor_scalar(
+                out=val[:], in0=cb[:, 4:5], scalar1=1.0 / TINY, scalar2=1.0, op0=ALU.mult, op1=ALU.min
             )
             c0 = 4 * (n % 2) + 2
             nc.tensor.matmul(out=misc[:, c0:c0 + 1], lhsT=onesm[:], rhs=val[:], start=True, stop=True)
-            st[("gcb", n)] = cb
 
-        def fin_gcopy(n):
+        def fin_gcopy(n, cb):
             c0 = 4 * (n % 2) + 2
-            nc.scalar.activation(out=st[("gcb", n)][:, 5:6], in_=misc[:, c0:c0 + 1], func=ACT.Copy)
+            nc.scalar.activation(out=cb[:, 5:6], in_=misc[:, c0:c0 + 1], func=ACT.Copy)
 
-        def fin_c(n, p):
-            rk = st[("res", p - 3)]
-            rg = st[("res", p - 1)]
+        def fin_c(n):
+            res = st[("res", 2 * n + 6)]
             ot = soft.tile([P, C], F32, name="ot%d" % n, tag="ot")
             nc.vector.tensor_scalar(
-                out=ot[:], in0=st[("vv", n)][:], scalar1=rk[:, 4:5], scalar2=rg[:, 5:6],
+                out=ot[:], in0=st[("vv", n)][:], scalar1=res[:, 4:5], scalar2=res[:, 5:6],
                 op0=ALU.mult, op1=ALU.mult,
             )
             o2 = out[n].rearrange("(k c) -> k c", c=C)
             nc.sync.dma_start(out=o2[0:112, :], in_=ot[0:112, :])
             nc.sync.dma_start(out=o2[112:127, :], in_=ot[112:127, :])
 
-        for p in range(-3, NU + 7):
+        for p in range(-3, NU + 6):
             na = img(p - 4)
-            nb = img(p - 6)
-            ncc = img(p - 8)
-            if ok(p - 1):
-                do_mx1(p - 1)
+            nb = img(p - 5)
+            ncc = img(p - 7)
             if ok(p + 2):
                 do_ss(p + 2, comb(p))
             if na is not None:
                 fin_nas(na)
+            if ok(p) and S_COLS > 0:
+                do_sreg(p)
             if ok(p):
                 do_n1(p)
                 if p % 2 == 1:
@@ -343,40 +355,42 @@ def tile_netvlad_kernel(tc, x, conv_w, conv_b, centroids, out):
             if ok(p - 2):
                 do_recip(p - 2)
                 do_ag(p - 2)
-            has_r = img(p - 5) is not None
-            has_g = img(p - 7) is not None
-            lo = 0 if ok(p + 2) else (4 if has_r else 5)
-            hi = 6 if has_g else (5 if has_r else 4)
+            lo = 0 if ok(p + 2) else 4
+            hi = 6 if img(p - 6) is not None else 4
             if hi > lo:
                 do_pow(p, lo, hi)
             if ok(p + 1):
                 do_n2u(p + 1)
+            if ok(p - 1):
+                do_add(p - 1)
             if ok(p):
                 do_regroup(p)
             if ok(p + 1):
                 do_b(p + 1)
             if ok(p - 1):
-                do_add(p - 1)
-            if ok(p - 2):
-                do_asum(p - 2)
-            if na is not None:
-                fin_stt(na)
-            if ncc is not None:
-                fin_c(ncc, p)
-            if ok(p):
-                do_q(p)
-            if ok(p - 1):
                 do_max(p - 1)
                 do_exp(p - 1)
+            if ok(p - 2):
+                do_asum(p - 2)
             if nb is not None:
-                fin_b(nb, p, comb(p + 1))
+                fin_b(nb, comb(p + 1))
+            if na is not None:
+                fin_stt(na)
+            if ok(p):
+                do_q(p)
             if ok(p + 3):
                 do_t(p + 3)
+            if p == -2:
+                setup_w()
+            if ok(p):
+                do_mx1(p)
+            if ncc is not None:
+                fin_c(ncc)
             if ok(p - 2):
                 do_qa(p - 2)
             if na is not None:
-                fin_sq(na, comb(p + 1))
+                fin_sq(na, comb(p + 2))
             if nb is not None:
-                fin_gcopy(nb)
+                fin_gcopy(nb, comb(p + 1))
             if ok(p - 2):
                 do_mx2(p - 2)

@@ -19,7 +19,7 @@ PX = 1024
 NU = 2 * N_IMG
 TINY = 1e-24
 FLOPS = 2 * 2 * N_IMG * 128 * C * PX
-S_COLS = 64
+S_COLS = 0
 
 
 def tile_netvlad_kernel(tc, x, conv_w, conv_b, centroids, out):

@@ -19,7 +19,7 @@ PX = 1024
 NU = 2 * N_IMG
 TINY = 1e-24
 FLOPS = 2 * 2 * N_IMG * 128 * C * PX
-S_COLS = 0
+S_COLS = 64
 
 
 def tile_netvlad_kernel(tc, x, conv_w, conv_b, centroids, out):
@@ -28,8 +28,8 @@ def tile_netvlad_kernel(tc, x, conv_w, conv_b, centroids, out):
         const = ctx.enter_context(tc.tile_pool(name="const", bufs=1))
         xpool = ctx.enter_context(tc.tile_pool(name="xpool", bufs=4))
         big = ctx.enter_context(tc.tile_pool(name="big", bufs=2))
-        keep = ctx.enter_context(tc.tile_pool(name="keep", bufs=4))
-        soft = ctx.enter_context(tc.tile_pool(name="soft", bufs=3))
+        keep = ctx.enter_context(tc.tile_pool(name="keep", bufs=5))
+        soft = ctx.enter_context(tc.tile_pool(name="soft", bufs=4))
         small = ctx.enter_context(tc.tile_pool(name="small", bufs=6))
         ps_r = ctx.enter_context(tc.psum_pool(name="ps_r", bufs=4))
         ps_b = ctx.enter_context(tc.psum_pool(name="ps_b", bufs=1))
@@ -328,7 +328,7 @@ def tile_netvlad_kernel(tc, x, conv_w, conv_b, centroids, out):
             nc.scalar.activation(out=cb[:, 5:6], in_=misc[:, c0:c0 + 1], func=ACT.Copy)
 
         def fin_c(n):
-            res = st[("res", 2 * n + 6)]
+            res = st[("res", 2 * n + 7)]
             ot = soft.tile([P, C], F32, name="ot%d" % n, tag="ot")
             nc.vector.tensor_scalar(
                 out=ot[:], in0=st[("vv", n)][:], scalar1=res[:, 4:5], scalar2=res[:, 5:6],
@@ -338,25 +338,25 @@ def tile_netvlad_kernel(tc, x, conv_w, conv_b, centroids, out):
             nc.sync.dma_start(out=o2[0:112, :], in_=ot[0:112, :])
             nc.sync.dma_start(out=o2[112:127, :], in_=ot[112:127, :])
 
-        for p in range(-3, NU + 6):
-            na = img(p - 4)
-            nb = img(p - 5)
-            ncc = img(p - 7)
+        for p in range(-3, NU + 7):
+            na = img(p - 5)
+            nb = img(p - 6)
+            ncc = img(p - 8)
             if ok(p + 2):
                 do_ss(p + 2, comb(p))
             if na is not None:
                 fin_nas(na)
             if ok(p) and S_COLS > 0:
                 do_sreg(p)
+            if ok(p - 3):
+                do_recip(p - 3)
+                do_ag(p - 3)
             if ok(p):
                 do_n1(p)
                 if p % 2 == 1:
                     load(p // 2 + 4)
-            if ok(p - 2):
-                do_recip(p - 2)
-                do_ag(p - 2)
             lo = 0 if ok(p + 2) else 4
-            hi = 6 if img(p - 6) is not None else 4
+            hi = 6 if img(p - 7) is not None else 4
             if hi > lo:
                 do_pow(p, lo, hi)
             if ok(p + 1):
@@ -370,8 +370,8 @@ def tile_netvlad_kernel(tc, x, conv_w, conv_b, centroids, out):
             if ok(p - 1):
                 do_max(p - 1)
                 do_exp(p - 1)
-            if ok(p - 2):
-                do_asum(p - 2)
+            if ok(p - 3):
+                do_asum(p - 3)
             if nb is not None:
                 fin_b(nb, comb(p + 1))
             if na is not None:
@@ -386,11 +386,11 @@ def tile_netvlad_kernel(tc, x, conv_w, conv_b, centroids, out):
                 do_mx1(p)
             if ncc is not None:
                 fin_c(ncc)
-            if ok(p - 2):
-                do_qa(p - 2)
+            if ok(p - 3):
+                do_qa(p - 3)
             if na is not None:
                 fin_sq(na, comb(p + 2))
             if nb is not None:
                 fin_gcopy(nb, comb(p + 1))
-            if ok(p - 2):
-                do_mx2(p - 2)
+            if ok(p - 3):
+                do_mx2(p - 3)

from contextlib import ExitStack

import concourse.mybir as mybir
from concourse.masks import make_identity

F32 = mybir.dt.float32
BF16 = mybir.dt.bfloat16
U32 = mybir.dt.uint32
U8 = mybir.dt.uint8
FP8X4 = mybir.dt.float8_e4m3fn_x4
ALU = mybir.AluOpType
ACT = mybir.ActivationFunctionType
AX = mybir.AxisListType

P = 128
N_IMG = 16
C = 512
PX = 1024
NU = 2 * N_IMG
TINY = 1e-24
FLOPS = 2 * 2 * N_IMG * 128 * C * PX
S_COLS = 64


def tile_netvlad_kernel(tc, x, conv_w, conv_b, centroids, out):
    nc = tc.nc
    with ExitStack() as ctx:
        const = ctx.enter_context(tc.tile_pool(name="const", bufs=1))
        xpool = ctx.enter_context(tc.tile_pool(name="xpool", bufs=4))
        big = ctx.enter_context(tc.tile_pool(name="big", bufs=2))
        keep = ctx.enter_context(tc.tile_pool(name="keep", bufs=5))
        soft = ctx.enter_context(tc.tile_pool(name="soft", bufs=4))
        small = ctx.enter_context(tc.tile_pool(name="small", bufs=6))
        ps_r = ctx.enter_context(tc.psum_pool(name="ps_r", bufs=4))
        ps_b = ctx.enter_context(tc.psum_pool(name="ps_b", bufs=1))
        ps_l = ctx.enter_context(tc.psum_pool(name="ps_l", bufs=1))
        ps_v = ctx.enter_context(tc.psum_pool(name="ps_v", bufs=1))
        ps_m = ctx.enter_context(tc.psum_pool(name="ps_m", bufs=1))
        ctx.enter_context(tc.manual_schedule())

        xs = {}

        def load(n, halves=False):
            if n >= N_IMG:
                return
            xt = xpool.tile([P, 4 * PX], BF16, name="xt%d" % n, tag="xt")
            if halves:
                src = x[n].rearrange("(q j) h w -> q j (h w)", j=4)
                dst = xt[:].rearrange("p (j w) -> p j w", j=4)
                for g in range(2):
                    nc.sync.dma_start(out=dst[:, :, 512 * g:512 * (g + 1)], in_=src[:, :, 512 * g:512 * (g + 1)])
            else:
                nc.sync.dma_start(out=xt[:], in_=x[n].rearrange("(q j) h w -> q (j h w)", j=4))
            xs[n] = xt

        load(0, halves=True)
        w_sb = const.tile([P, C], BF16, name="w_sb")
        nc.sync.dma_start(out=w_sb[:], in_=conv_w)
        b_bc = const.tile([P, 128], BF16, name="b_bc")
        nc.sync.dma_start(out=b_bc[:], in_=conv_b.partition_broadcast(P))
        cent = const.tile([P, C], BF16, name="cent")
        nc.sync.dma_start(out=cent[:], in_=centroids)
        load(1)
        load(2)
        load(3)

        ident = const.tile([P, P], F32, name="ident")
        make_identity(nc, ident[:])
        expo = const.tile([P, 6], F32, name="expo")
        nc.gpsimd.memset(expo[:], -0.5)
        onesm = const.tile([P, P], F32, name="onesm")
        nc.vector.tensor_scalar(
            out=onesm[:], in0=ident[:, 127:128].to_broadcast([P, P]),
            scalar1=-1.0, scalar2=1.0, op0=ALU.mult, op1=ALU.add,
        )
        junk = const.tile([P, C], BF16, name="junk")
        junk3 = const.tile([P, 2], F32, name="junk3")
        misc = ps_m.tile([P, 512], F32, name="misc")

        w_codes = const.tile([P, 128], U32, name="w_codes", align_bytes=64)
        w_scales = const.tile([P, 128], U8, name="w_scales", align_bytes=64)

        def setup_w():
            w32 = w_sb[:].bitcast(F32)
            w_t = ps_l.tile([P, 512], F32, name="w_t", tag="L")
            for v in range(2):
                nc.tensor.transpose(w_t[:, v * 128:(v + 1) * 128], w32[:, v:256:2], ident[:])
            wg = const.tile([P, C], BF16, name="wg", align_bytes=64)
            nc.vector.tensor_copy(
                out=wg[:].bitcast(F32).rearrange("p (k v) -> p k v", v=2),
                in_=w_t[:, 0:256].rearrange("p (v k) -> p k v", v=2),
            )
            nc.vector.quantize_mx(out=w_codes[:].bitcast(FP8X4), scales=w_scales[:], in_=wg[:])

        st = {}

        def ok(s):
            return 0 <= s < NU

        def img(num):
            if num % 2 == 0 and 0 <= num // 2 < N_IMG:
                return num // 2
            return None

        def r16(s, u):
            return st[("R", s)][u][:].bitcast(BF16).rearrange("p (c e) -> p c e", e=2)

        def do_t(s):
            n, g = divmod(s, 2)
            x32 = xs[n][:].bitcast(F32)
            banks = []
            for u in range(2):
                ru = ps_r.tile([P, 512], F32, name="r%d_%d" % (s, u), tag="R")
                for j in range(4):
                    col = j * 512 + 256 * g + 128 * u
                    nc.tensor.transpose(ru[:, j * 128:(j + 1) * 128], x32[:, col:col + 128], ident[:])
                banks.append(ru)
            st[("R", s)] = banks

        def comb(p):
            if ("cb", p) not in st:
                st[("cb", p)] = small.tile([P, 6], F32, name="cb%d" % p, tag="cb")
            return st[("cb", p)]

        def do_ss(s, cb):
            for u in range(2):
                for e in range(2):
                    t = 2 * u + e
                    nc.scalar.activation(
                        out=junk[:], in_=r16(s, u)[:, :, e], func=ACT.Square,
                        accum_out=cb[:, t:t + 1],
                    )

        def do_pow(p, lo, hi):
            cb = st[("cb", p)]
            cbc = small.tile([P, 6], F32, name="cbc%d" % p, tag="cbc")
            nc.gpsimd.tensor_scalar(
                out=cbc[:, lo:hi], in0=cb[:, lo:hi], scalar1=TINY, scalar2=None, op0=ALU.max
            )
            res = small.tile([P, 6], F32, name="res%d" % p, tag="res")
            nc.gpsimd.tensor_tensor(out=res[:, lo:hi], in0=cbc[:, lo:hi], in1=expo[:, lo:hi], op=ALU.pow)
            st[("res", p)] = res

        def do_n2u(s):
            rn = st[("res", s - 2)]
            xu = big.tile([P, 2048], BF16, name="xu%d" % s, tag="xu")
            for u in range(2):
                for e in range(2):
                    t = 2 * u + e
                    nc.scalar.activation(
                        out=xu[:, t * 512:(t + 1) * 512], in_=r16(s, u)[:, :, e], func=ACT.Copy,
                        scale=rn[:, t:t + 1],
                    )
            st[("xu", s)] = xu

        def do_b(s):
            rn = st[("res", s - 2)]
            bt = ps_b.tile([P, 512], F32, name="bt%d" % s, tag="B")
            for t in range(4):
                nc.tensor.transpose(
                    bt[:, t * 128:(t + 1) * 128], rn[:, t:t + 1].to_broadcast([P, P]), ident[:]
                )
            st[("B", s)] = bt

        def qin_of(s):
            if ("qin", s) not in st:
                st[("qin", s)] = big.tile([P, 4096], BF16, name="qin%d" % s, tag="qin", align_bytes=64)
            return st[("qin", s)]

        def regroup_views(s):
            dst = qin_of(s)[:, 2048:4096].rearrange("p (c i t) -> p c t i", i=4, t=4)
            src = st[("xu", s)][:].rearrange("p (t c i) -> p c t i", t=4, i=4)
            return dst, src

        def do_regroup(s):
            dst, src = regroup_views(s)
            cut = (C - S_COLS) // 4
            nc.vector.tensor_copy(out=dst[:, 0:cut], in_=src[:, 0:cut])

        def do_sreg(s):
            dst, src = regroup_views(s)
            cut = (C - S_COLS) // 4
            nc.scalar.copy(out=dst[:, cut:128], in_=src[:, cut:128])

        def do_n1(s):
            n, g = divmod(s, 2)
            qin = qin_of(s)
            cg4 = qin[:, 0:2048].rearrange("p (t q j) -> p t q j", t=4, j=4)
            xv = xs[n][:].rearrange("p (j g u q e) -> p g u e q j", j=4, g=2, u=2, e=2)
            b3 = st[("B", s)][:].rearrange("p (t q) -> p t q", t=4)
            for u in range(2):
                nc.vector.tensor_tensor(
                    out=cg4[:, 2 * u:2 * u + 2],
                    in0=xv[:, g, u],
                    in1=b3[:, 2 * u:2 * u + 2, :].unsqueeze(3).to_broadcast([P, 2, 128, 4]),
                    op=ALU.mult,
                )

        def do_q(s):
            qc = keep.tile([P, 1024], U32, name="qc%d" % s, tag="qc", align_bytes=64)
            qs = keep.tile([P, 1024], U8, name="qs%d" % s, tag="qs", align_bytes=64)
            nc.vector.quantize_mx(out=qc[:].bitcast(FP8X4), scales=qs[:], in_=st[("qin", s)][:])
            st[("q", s)] = (qc, qs)

        def do_mx1(s):
            xcc, xcs = st[("q", s)]
            lt = ps_l.tile([P, 512], F32, name="lt%d" % s, tag="L")
            for t in range(4):
                cols = slice(t * 128, (t + 1) * 128)
                nc.tensor.matmul_mx(
                    out=lt[:, cols],
                    lhsT=xcc[:, cols].bitcast(FP8X4), lhsT_scale=xcs[:, cols],
                    rhs=w_codes[:].bitcast(FP8X4), rhs_scale=w_scales[:],
                    start=True, stop=True,
                )
            st[("L", s)] = lt

        def do_add(s):
            z = soft.tile([P, 512], F32, name="z%d" % s, tag="z")
            nc.vector.tensor_tensor(
                out=z[:].rearrange("p (t k) -> p t k", t=4),
                in0=st[("L", s)][:].rearrange("p (t k) -> p t k", t=4),
                in1=b_bc[:].unsqueeze(1).to_broadcast([P, 4, 128]), op=ALU.add,
            )
            st[("z", s)] = z

        def do_max(s):
            negm = small.tile([P, 4], F32, name="negm%d" % s, tag="negm")
            nc.vector.tensor_reduce(
                out=negm[:], in_=st[("z", s)][:].rearrange("p (t k) -> p t k", t=4),
                axis=AX.X, op=ALU.max, negate=True,
            )
            st[("negm", s)] = negm

        def do_exp(s):
            z = st[("z", s)]
            negm = st[("negm", s)]
            cb = small.tile([P, 4], F32, name="sums%d" % s, tag="sums")
            st[("sums", s)] = cb
            ex = soft.tile([P, 512], F32, name="ex%d" % s, tag="ex")
            for t in range(4):
                cols = slice(t * 128, (t + 1) * 128)
                nc.scalar.activation(
                    out=ex[:, cols], in_=z[:, cols], func=ACT.Exp,
                    bias=negm[:, t:t + 1], scale=1.0, accum_out=cb[:, t:t + 1],
                )
            st[("ex", s)] = ex

        def do_recip(s):
            rs = small.tile([P, 4], F32, name="rs%d" % s, tag="rs")
            nc.vector.reciprocal(out=rs[:], in_=st[("sums", s)][:])
            st[("rs", s)] = rs

        def do_asum(s):
            n, g = divmod(s, 2)
            ex = st[("ex", s)]
            rs = st[("rs", s)]
            col = 4 * (n % 2) + g
            for t in range(4):
                nc.tensor.matmul(
                    out=misc[:, col:col + 1], lhsT=ex[:, t * 128:(t + 1) * 128],
                    rhs=rs[:, t:t + 1], start=(t == 0), stop=(t == 3),
                )

        def do_ag(s):
            rs = st[("rs", s)]
            ag = big.tile([P, 512], BF16, name="ag%d" % s, tag="ag", align_bytes=64)
            eng = nc.vector if s >= NU - 2 else nc.gpsimd
            eng.tensor_tensor(
                out=ag[:].rearrange("p (k t) -> p k t", t=4),
                in0=st[("ex", s)][:].rearrange("p (t k) -> p k t", t=4),
                in1=rs[:, 0:4].unsqueeze(1).to_broadcast([P, 128, 4]), op=ALU.mult,
            )
            st[("ag", s)] = ag

        def do_qa(s):
            ac = big.tile([P, 128], U32, name="ac%d" % s, tag="ac", align_bytes=64)
            asc = big.tile([P, 128], U8, name="asc%d" % s, tag="asc", align_bytes=64)
            nc.vector.quantize_mx(out=ac[:].bitcast(FP8X4), scales=asc[:], in_=st[("ag", s)][:])
            st[("a", s)] = (ac, asc)

        def do_mx2(s):
            n, g = divmod(s, 2)
            if g == 0:
                st[("V", n)] = ps_v.tile([P, 512], F32, name="vl%d" % n, tag="V")
            ac, asc = st[("a", s)]
            qc, qs = st[("q", s)]
            nc.tensor.matmul_mx(
                out=st[("V", n)][:],
                lhsT=ac[:].bitcast(FP8X4), lhsT_scale=asc[:],
                rhs=qc[:, 512:1024].bitcast(FP8X4), rhs_scale=qs[:, 512:1024],
                start=(g == 0), stop=(g == 1),
            )

        def fin_nas(n):
            c0 = 4 * (n % 2)
            nas = small.tile([P, 1], F32, name="nas%d" % n, tag="nas")
            nc.scalar.activation(
                out=junk3[:], in_=misc[:, c0:c0 + 2], func=ACT.Copy, scale=-1.0, accum_out=nas[:]
            )
            st[("nas", n)] = nas

        def fin_stt(n):
            nas = st[("nas", n)]
            vv = soft.tile([P, C], F32, name="vv%d" % n, tag="vv")
            nc.vector.scalar_tensor_tensor(
                out=vv[:].rearrange("p (q j) -> p q j", j=4),
                in0=cent[:].rearrange("p (q j) -> p q j", j=4),
                scalar=nas[:, 0:1],
                in1=st[("V", n)][:].rearrange("p (j q) -> p q j", j=4),
                op0=ALU.mult, op1=ALU.add,
            )
            st[("vv", n)] = vv

        def fin_sq(n, cb):
            nc.scalar.activation(out=junk[:], in_=st[("vv", n)][:], func=ACT.Square, accum_out=cb[:, 4:5])

        def fin_b(n, cb):
            val = small.tile([P, 1], F32, name="val%d" % n, tag="val")
            nc.vector.tensor_scalar(
                out=val[:], in0=cb[:, 4:5], scalar1=1.0 / TINY, scalar2=1.0, op0=ALU.mult, op1=ALU.min
            )
            c0 = 4 * (n % 2) + 2
            nc.tensor.matmul(out=misc[:, c0:c0 + 1], lhsT=onesm[:], rhs=val[:], start=True, stop=True)

        def fin_gcopy(n, cb):
            c0 = 4 * (n % 2) + 2
            nc.scalar.activation(out=cb[:, 5:6], in_=misc[:, c0:c0 + 1], func=ACT.Copy)

        def fin_c(n):
            res = st[("res", 2 * n + 7)]
            ot = soft.tile([P, C], F32, name="ot%d" % n, tag="ot")
            nc.vector.tensor_scalar(
                out=ot[:], in0=st[("vv", n)][:], scalar1=res[:, 4:5], scalar2=res[:, 5:6],
                op0=ALU.mult, op1=ALU.mult,
            )
            o2 = out[n].rearrange("(k c) -> k c", c=C)
            nc.sync.dma_start(out=o2[0:112, :], in_=ot[0:112, :])
            nc.sync.dma_start(out=o2[112:127, :], in_=ot[112:127, :])

        for p in range(-3, NU + 7):
            na = img(p - 5)
            nb = img(p - 6)
            ncc = img(p - 8)
            if ok(p + 2):
                do_ss(p + 2, comb(p))
            if na is not None:
                fin_nas(na)
            if ok(p) and S_COLS > 0:
                do_sreg(p)
            if ok(p - 3):
                do_recip(p - 3)
                do_ag(p - 3)
            if ok(p):
                do_n1(p)
                if p % 2 == 1:
                    load(p // 2 + 4)
            lo = 0 if ok(p + 2) else 4
            hi = 6 if img(p - 7) is not None else 4
            if hi > lo:
                do_pow(p, lo, hi)
            if ok(p + 1):
                do_n2u(p + 1)
            if ok(p - 1):
                do_add(p - 1)
            if ok(p):
                do_regroup(p)
            if ok(p + 1):
                do_b(p + 1)
            if ok(p - 1):
                do_max(p - 1)
                do_exp(p - 1)
            if ok(p - 3):
                do_asum(p - 3)
            if nb is not None:
                fin_b(nb, comb(p + 1))
            if na is not None:
                fin_stt(na)
            if ok(p):
                do_q(p)
            if ok(p + 3):
                do_t(p + 3)
            if p == -2:
                setup_w()
            if ok(p):
                do_mx1(p)
            if ncc is not None:
                fin_c(ncc)
            if ok(p - 3):
                do_qa(p - 3)
            if na is not None:
                fin_sq(na, comb(p + 2))
            if nb is not None:
                fin_gcopy(nb, comb(p + 1))
            if ok(p - 3):
                do_mx2(p - 3)
